import numpy as np
import ml_dtypes


def mxq(x, axis, fmt="e4m3"):
    dtype, down = {"e4m3": (ml_dtypes.float8_e4m3fn, 7), "e5m2": (ml_dtypes.float8_e5m2, 14)}[fmt]
    v = np.moveaxis(np.asarray(x, np.float32).astype(ml_dtypes.bfloat16).astype(np.float64), axis, -1)
    blocks = v.reshape(v.shape[:-1] + (-1, 32))
    amax = np.abs(blocks).max(-1, keepdims=True)
    byte = np.maximum(np.where(amax > 0, np.frexp(amax)[1] - 1 + 127, 0) - down, 1)
    scale = np.exp2(byte - 127.0)
    codes = (blocks / scale).astype(np.float32).astype(dtype).astype(np.float64)
    return np.moveaxis((codes * scale).reshape(v.shape), -1, axis)


WIDE = False


def mx_kscale(k):
    if not WIDE:
        return np.ones(k)
    levels = np.array([10, -10, 5, -5, 0])
    if k % 512:
        return np.exp2(np.random.permutation(np.resize(levels, k // 32))).repeat(32)
    a = np.empty((k // 512, 16))
    for p in range(k // 512):
        a[p, :8] = np.random.permutation(np.resize(levels, 8))
        for g in range(8):
            far = levels[np.abs(levels - a[p, g]) >= 10]
            a[p, g + 8] = far[np.random.randint(len(far))]
    return np.exp2(a.ravel()).repeat(32)


BF16 = ml_dtypes.bfloat16


def bf(x):
    return np.asarray(x, np.float32).astype(BF16)


def f64(x):
    return np.asarray(x).astype(np.float64)


E2M1 = np.array([0.0, 0.5, 1.0, 1.5, 2.0, 3.0, 4.0, 6.0, -0.0, -0.5, -1.0, -1.5, -2.0, -3.0, -4.0, -6.0])


def pack_weight(w, fmt):
    k, n = w.shape
    w = f64(bf(w)).reshape(k // 32, 32, n)
    amax = np.abs(w).max(1)
    if fmt == "e4m3":
        byte = np.frexp(amax)[1] - 1 + 127 - 7
    else:
        mant, ex = np.frexp(amax / 6.0)
        byte = np.where(mant > 0.5, ex, ex - 1) + 127
    byte = np.clip(np.where(amax > 0, byte, 1), 1, 254)
    scaled = (w * np.exp2(127.0 - byte)[:, None, :]).reshape(k, n).astype(np.float32)
    by_word = np.ascontiguousarray(scaled.reshape(k // 512, 128, 4, n).transpose(0, 1, 3, 2))
    if fmt == "e4m3":
        words = by_word.astype(ml_dtypes.float8_e4m3fn).view(np.uint8)
    else:
        c = by_word.astype(ml_dtypes.float4_e2m1fn).view(np.uint8) & 0xF
        words = c[..., 0::2] | (c[..., 1::2] << 4)
    return np.ascontiguousarray(words), np.ascontiguousarray(byte.astype(np.uint8).reshape(k // 512, 16, n))


def unpack_weight(words, scales, fmt):
    g, p, n, _ = words.shape
    if fmt == "e4m3":
        vals = np.ascontiguousarray(words).view(ml_dtypes.float8_e4m3fn).astype(np.float64)
    else:
        nib = np.empty((g, p, n, 4), np.uint8)
        nib[..., 0::2] = words & 0xF
        nib[..., 1::2] = words >> 4
        vals = E2M1[nib]
    vals = vals * np.repeat(np.exp2(scales.astype(np.float64) - 127.0), 8, axis=1)[..., None]
    return vals.transpose(0, 1, 3, 2).reshape(g * 512, n)
def pack4(w):
    words, scales = pack_weight(w, "e2m1")
    return words.reshape(words.shape[0], 128, -1), scales


def unpack4(words, scales):
    return unpack_weight(words.reshape(words.shape[0], 128, -1, 2), scales, "e2m1")


B, HALF, MID = 512, 512, 2048
D = 2 * HALF


def draw0():
    s, t = mx_kscale(MID), mx_kscale(MID)
    x = bf(np.random.standard_normal((B, D)))
    h3 = bf(np.maximum(np.random.standard_normal((B, MID)), 0.0) * s)
    W4_words, W4_scales = pack4(np.random.standard_normal((MID, MID)) * np.sqrt(2.0 / MID) / s[:, None] * t)
    b4 = bf(np.random.standard_normal(MID) * 0.2 * t)
    W5_words, W5_scales = pack4(np.random.standard_normal((MID, HALF)) * np.sqrt(2.0 / MID) / t[:, None])
    b5 = bf(np.random.standard_normal(HALF) * 0.2)
    return {"x": x,
            "h3": h3,
            "W4_words": W4_words,
            "W4_scales": W4_scales,
            "b4": b4,
            "W5_words": W5_words,
            "W5_scales": W5_scales,
            "b5": b5}


def core(x, h3, W4_words, W4_scales, b4, W5_words, W5_scales, b5):
    x = f64(x)
    even = x[:, 0::2]
    odd = x[:, 1::2]
    h4 = np.maximum((mxq(f64(h3), 1, "e4m3") @ unpack4(W4_words, W4_scales)) + f64(b4), 0.0)
    m = (mxq(h4, 1, "e4m3") @ unpack4(W5_words, W5_scales)) + f64(b5)
    transformed = even + m
    return np.stack([transformed, odd], axis=2).reshape(B, -1)


def e4m3fn_bytes(y):
    return np.clip(np.asarray(y, np.float64), -448.0, 448.0).astype(np.float32).astype(ml_dtypes.float8_e4m3fn).view(np.uint8)


def e4m3fn_values(b):
    return np.asarray(b, np.uint8).view(ml_dtypes.float8_e4m3fn).astype(np.float64)


def setup_inputs():
    d = draw0()
    x0 = np.asarray(d['h3']).astype(np.float64)
    s = (np.max(np.abs(x0), axis=(0,), keepdims=True) / 448.0).astype(np.float32)
    out = {}
    for k, v in d.items():
        if k == 'h3':
            out['h3_bytes'] = e4m3fn_bytes(x0 / s.astype(np.float64))
            out['h3_scale'] = s
        else:
            out[k] = v
    return out


def reference(x, h3_bytes, h3_scale, W4_words, W4_scales, b4, W5_words, W5_scales, b5):
    return core(x, e4m3fn_values(h3_bytes) * h3_scale.astype(np.float64), W4_words, W4_scales, b4, W5_words, W5_scales, b5)

@@ -1,0 +1,360 @@
+from contextlib import ExitStack
+
+import concourse.mybir as mybir
+from concourse.masks import make_identity
+
+B, HALF, MID = 512, 512, 2048
+FLOPS = 2 * B * MID * MID + 2 * B * MID * HALF
+
+P = 128
+TT = B // P
+NG = MID // 512
+F32 = mybir.dt.float32
+BF16 = mybir.dt.bfloat16
+U8 = mybir.dt.uint8
+U32 = mybir.dt.uint32
+I32 = mybir.dt.int32
+FP8 = mybir.dt.float8_e4m3fn
+FP8X4 = mybir.dt.float8_e4m3fn_x4
+FP4X4 = mybir.dt.float4_e2m1fn_x4
+ALU = mybir.AluOpType
+ACT = mybir.ActivationFunctionType
+
+NM = 3
+TILES = [(g, j) for j in range(4) for g in range(2)] + [(2, j) for j in range(4)]
+SWEEP = 6
+EXIT_V = (1, 3, 5, 7, 9)
+
+
+def tile_additivecoupling_pa_w4_kernel(
+    tc, x, h3_bytes, h3_scale, W4_words, W4_scales, b4, W5_words, W5_scales, b5, out
+):
+    nc = tc.nc
+    with ExitStack() as ctx:
+        keep = ctx.enter_context(tc.tile_pool(name="keep", bufs=1))
+        work = ctx.enter_context(tc.tile_pool(name="work", bufs=2))
+        psum = ctx.enter_context(tc.psum_pool(name="psum", bufs=1))
+        ctx.enter_context(tc.manual_schedule())
+
+        ident = keep.tile([P, P], F32, name="ident")
+        make_identity(nc, ident[:])
+        w4s = keep.tile([P, NG, MID], U8, name="w4s", align_bytes=64)
+        w5s = keep.tile([P, NG, HALF], U8, name="w5s", align_bytes=64)
+        nc.vector.memset(w4s[:].rearrange("p g n -> p (g n)").bitcast(I32), 0)
+        nc.vector.memset(w5s[:].rearrange("p g n -> p (g n)").bitcast(I32), 0)
+        b4rows = keep.tile([P, P], BF16, name="b4rows")
+        nc.gpsimd.memset(b4rows[:], 0.0)
+        warm = keep.tile([P, 1], F32, name="warm")
+        nc.gpsimd.memset(warm[:], 0.0)
+        warm2 = keep.tile([P, 1], F32, name="warm2")
+        nc.scalar.activation(out=warm2[:], in_=warm[:], func=ACT.Relu)
+
+        h3v = h3_bytes.rearrange("(p i) k -> p i k", i=TT)
+        sc, hb, w4a = [], [], []
+        w4b = keep.tile([P, NG, 4096 - 1024 * NM], U8, name="w4b", align_bytes=64)
+        w5 = keep.tile([P, NG, 1024], U8, name="w5", align_bytes=64)
+        for g in range(NG):
+            s_g = keep.tile([P, 512], F32, name=f"sc{g}", align_bytes=64)
+            h_g = keep.tile([P, TT, 512], U8, name=f"hb{g}", align_bytes=64)
+            a_g = keep.tile([P, 512 * 2 * NM], U8, name=f"w4a{g}", align_bytes=64)
+            sc.append(s_g)
+            hb.append(h_g)
+            w4a.append(a_g)
+        def load_h3(g):
+            k_cols = slice(512 * g, 512 * (g + 1))
+            nc.sync.dma_start(out=sc[g][:], in_=h3_scale[:, k_cols].rearrange("o k -> (o k)").partition_broadcast(P))
+            nc.sync.dma_start(out=hb[g][:], in_=h3v[:, :, k_cols])
+
+        def load_w4(g):
+            nc.sync.dma_start(out=w4a[g][:].bitcast(I32), in_=W4_words[g, :, 0 : 1024 * NM].bitcast(I32))
+
+        load_h3(0)
+        load_h3(1)
+        for q in range(4):
+            nc.sync.dma_start(
+                out=w4s[32 * q : 32 * q + 4, :, :].bitcast(I32),
+                in_=W4_scales[:, 4 * q : 4 * q + 4, :].rearrange("g r n -> r g n").bitcast(I32),
+            )
+        load_w4(0)
+        load_h3(2)
+        load_w4(1)
+        load_h3(3)
+        load_w4(2)
+        load_w4(3)
+        nc.sync.dma_start(out=b4rows[0:16, :], in_=b4.rearrange("(c p) -> c p", p=P))
+        nc.sync.dma_start(out=w4b[:].bitcast(I32), in_=W4_words[:, :, 1024 * NM :].rearrange("g p n -> p g n").bitcast(I32))
+        b4bc = keep.tile([P, 512 * (NG - NM)], BF16, name="b4bc")
+        nc.sync.dma_start(out=b4bc[:], in_=b4[512 * NM :].partition_broadcast(P))
+        for q in range(4):
+            nc.sync.dma_start(
+                out=w5s[32 * q : 32 * q + 4, :, :].bitcast(I32),
+                in_=W5_scales[:, 4 * q : 4 * q + 4, :].rearrange("g r n -> r g n").bitcast(I32),
+            )
+        nc.sync.dma_start(out=w5[:].bitcast(I32), in_=W5_words.rearrange("g p n -> p g n").bitcast(I32))
+        b5bc = keep.tile([P, HALF], BF16, name="b5bc")
+        nc.sync.dma_start(out=b5bc[:], in_=b5.partition_broadcast(P))
+        xt = keep.tile([P, TT, 2 * HALF], BF16, name="xt")
+        nc.sync.dma_start(out=xt[:], in_=x.rearrange("(p i) c -> p i c", i=TT))
+
+        pair = keep.tile([P, TT, 2, HALF], F32, name="pair")
+        for i in range(TT):
+            nc.gpsimd.tensor_tensor(out=pair[:, i, 0, :], in0=xt[:, i, 0::2], in1=b5bc[:], op=ALU.add)
+            nc.gpsimd.tensor_scalar(
+                out=pair[:, i, 1, :], in0=xt[:, i, 1::2], scalar1=1.0, scalar2=0.0, op0=ALU.mult, op1=ALU.add
+            )
+
+        h3g, h3q, h3s, prods = [], [], [], {}
+        for g in range(NG):
+            t_g = work.tile([P, B, 4], BF16, name="h3g", tag="h3g", bufs=2, align_bytes=64)
+            q_g = keep.tile([P, B], U32, name=f"h3q{g}", align_bytes=64)
+            s_g = keep.tile([P, B], U8, name=f"h3s{g}", align_bytes=64)
+            h3g.append(t_g)
+            h3q.append(q_g)
+            h3s.append(s_g)
+
+        def product(g, i):
+            t = work.tile([P, 512], BF16, name="prod", tag="prod", bufs=6, align_bytes=64)
+            nc.vector.tensor_tensor(out=t[:], in0=hb[g][:, i, :].bitcast(FP8), in1=sc[g][:], op=ALU.mult)
+            prods[g, i] = t
+
+        def transpose_pair(g, half):
+            bank = psum.tile([P, 2, 2, P], F32, name="tr", tag="tr", bufs=2)
+            for ii in range(2):
+                words = prods[g, 2 * half + ii][:].bitcast(F32)
+                for u in range(2):
+                    nc.tensor.transpose(bank[:, ii, u, :], words[:, u::2], ident[:])
+            dst = h3g[g][:, 256 * half : 256 * (half + 1), :].rearrange("p c t -> p (c t)").bitcast(F32)
+            nc.scalar.copy(
+                out=dst.rearrange("p (i m u) -> p i m u", i=2, u=2), in_=bank[:].rearrange("p i u m -> p i m u")
+            )
+
+        def quantise_h3(g):
+            cols = slice(0, B)
+            nc.vector.quantize_mx(
+                out=h3q[g][:, cols].bitcast(FP8X4),
+                scales=h3s[g][:, cols],
+                in_=h3g[g][:, cols, :].rearrange("p c t -> p (c t)"),
+            )
+
+        acc = {}
+
+        def pass1(n, g):
+            if g == 0:
+                bank = psum.tile([P, B], F32, name="acc", tag=f"b{n % 6}", bufs=1)
+                acc[n] = bank
+            c = 4 * TILES[n][0] + TILES[n][1]
+            w = w4a[g][:, 256 * c : 256 * (c + 1)]
+            nc.tensor.matmul_mx(
+                out=acc[n][:],
+                lhsT=w.bitcast(FP4X4),
+                lhsT_scale=w4s[:, g, P * c : P * (c + 1)],
+                rhs=h3q[g][:].bitcast(FP8X4),
+                rhs_scale=h3s[g][:],
+                start=(g == 0),
+                stop=(g == NG - 1),
+            )
+
+        b4t = keep.tile([P, 16], F32, name="b4t")
+        h4n = keep.tile([P, NM, 4, B], BF16, name="h4n", align_bytes=64)
+        h4p = []
+        for j in range(4):
+            t_j = keep.tile([P, NM, B], BF16, name=f"h4p{j}", align_bytes=64)
+            h4p.append(t_j)
+
+        def exit1(n):
+            g, j = TILES[n]
+            c = 4 * g + j
+            if n in EXIT_V:
+                nc.vector.tensor_scalar(
+                    out=h4p[j][:, g, :], in0=acc[n][:], scalar1=b4t[:, c : c + 1], scalar2=0.0, op0=ALU.add, op1=ALU.max
+                )
+            else:
+                nc.scalar.activation(out=h4p[j][:, g, :], in_=acc[n][:], func=ACT.Relu, bias=b4t[:, c : c + 1])
+            moved = {0: None, 1: slice(0, 2), 2: slice(2, 3)}[g]
+            if moved is not None:
+                for s in range(4):
+                    nc.sync.dma_start(out=h4n[32 * j : 32 * (j + 1), moved, s, :], in_=h4p[j][s:P:4, moved, :])
+
+        h4q, h4s = [], []
+        for g in range(NG):
+            q_g = keep.tile([P, B], U32, name=f"h4q{g}", align_bytes=64)
+            s_g = keep.tile([P, B], U8, name=f"h4s{g}", align_bytes=64)
+            h4q.append(q_g)
+            h4s.append(s_g)
+
+        inter = {}
+
+        def interleave(g, copy, lo, hi):
+            if g not in inter:
+                t = work.tile([P, B, 4], BF16, name="h4i", tag="h4i", bufs=3, align_bytes=64)
+                inter[g] = t
+            copy(out=inter[g][:, lo:hi, :], in_=h4n[:, g, :, lo:hi].rearrange("p t c -> p c t"))
+
+        def quantise_h4(g, lo=0, hi=B):
+            nc.vector.quantize_mx(
+                out=h4q[g][:, lo:hi].bitcast(FP8X4),
+                scales=h4s[g][:, lo:hi],
+                in_=inter[g][:, lo:hi, :].rearrange("p c t -> p (c t)"),
+            )
+
+        h4t = {}
+
+        def group_tokens(i):
+            o = 3
+            bank = psum.tile([P, 512], F32, name="acc", tag=f"b{i % 2}", bufs=1)
+            cols = slice(P * i, P * (i + 1))
+            for g in range(NG):
+                nc.tensor.matmul_mx(
+                    out=bank[:],
+                    lhsT=h3q[g][:, cols].bitcast(FP8X4),
+                    lhsT_scale=h3s[g][:, cols],
+                    rhs=w4b[:, g, 1024 * (o - NM) : 1024 * (o - NM + 1)].bitcast(FP4X4),
+                    rhs_scale=w4s[:, g, 512 * o : 512 * (o + 1)],
+                    start=(g == 0),
+                    stop=(g == NG - 1),
+                )
+            return bank
+
+        def add_b4(i, bank):
+            t = work.tile([P, 512], BF16, name="h4t", tag="h4t", bufs=4, align_bytes=64)
+            order = "q (p u e) -> q u p e"
+            nc.vector.tensor_tensor(
+                out=t[:].rearrange("q (u p e) -> q u p e", u=2, e=2),
+                in0=bank[:].rearrange(order, u=2, e=2),
+                in1=b4bc[:].rearrange(order, u=2, e=2),
+                op=ALU.add,
+            )
+            h4t[i] = t
+
+        turned = {}
+
+        def turn_tokens(i):
+            bank = psum.tile([P, 2, P], F32, name="tr", tag="tr", bufs=2)
+            words = h4t[i][:].bitcast(F32)
+            for u in range(2):
+                nc.tensor.transpose(bank[:, u, :], words[:, P * u : P * (u + 1)], ident[:])
+            r = work.tile([P, P, 4], BF16, name="h4r", tag="h4r", bufs=4, align_bytes=64)
+            nc.scalar.activation(
+                out=r[:].rearrange("p m (u e) -> p m u e", u=2),
+                in_=bank[:].rearrange("p u m -> p (u m)").bitcast(BF16).rearrange("p (u m e) -> p m u e", u=2, e=2),
+                func=ACT.Relu,
+            )
+            turned[i] = r
+
+        def quantise_turned(i):
+            cols = slice(P * i, P * (i + 1))
+            nc.vector.quantize_mx(
+                out=h4q[3][:, cols].bitcast(FP8X4),
+                scales=h4s[3][:, cols],
+                in_=turned[i][:].rearrange("p m t -> p (m t)"),
+            )
+
+        acc2 = {}
+
+        def pass2(i, g):
+            if g == 0:
+                bank = psum.tile([P, HALF], F32, name="acc", tag=f"b{2 + i}", bufs=1)
+                acc2[i] = bank
+            cols = slice(P * i, P * (i + 1))
+            nc.tensor.matmul_mx(
+                out=acc2[i][:],
+                lhsT=h4q[g][:, cols].bitcast(FP8X4),
+                lhsT_scale=h4s[g][:, cols],
+                rhs=w5[:, g, :].bitcast(FP4X4),
+                rhs_scale=w5s[:, g, :],
+                start=(g == 0),
+                stop=(g == NG - 1),
+            )
+
+        outv = out.rearrange("(p i) c -> p i c", i=TT)
+
+        outt = []
+        for i in range(TT):
+            o_i = keep.tile([P, HALF, 2], F32, name=f"o{i}")
+            outt.append(o_i)
+
+        def finish_add(i):
+            nc.vector.tensor_tensor(out=pair[:, i, 0, :], in0=acc2[i][:], in1=pair[:, i, 0, :], op=ALU.add)
+
+        def out_pairs(i, copy, lo, hi):
+            copy(out=outt[i][:, lo:hi, :], in_=pair[:, i, :, lo:hi].rearrange("p r j -> p j r"))
+            if hi == HALF:
+                nc.sync.dma_start(out=outv[:, i, :], in_=outt[i][:].rearrange("p j r -> p (j r)"))
+
+        def turn_b4():
+            b4f = keep.tile([P, P], F32, name="b4f")
+            nc.vector.tensor_copy(out=b4f[:], in_=b4rows[:])
+            b4bank = psum.tile([P, P], F32, name="tr", tag="tr", bufs=2)
+            nc.tensor.transpose(b4bank[:], b4f[:], ident[:])
+            nc.scalar.copy(out=b4t[:], in_=b4bank[:, 0:16])
+
+        for g in range(NG):
+            product(g, 0)
+            product(g, 1)
+            transpose_pair(g, 0)
+            product(g, 2)
+            if g > 0:
+                quantise_h3(g - 1)
+            product(g, 3)
+            transpose_pair(g, 1)
+            if g > 0:
+                for n in range(SWEEP):
+                    pass1(n, g - 1)
+            if g == 2:
+                turn_b4()
+        quantise_h3(NG - 1)
+        for n in range(SWEEP):
+            pass1(n, NG - 1)
+            exit1(n)
+        V, S = nc.vector.tensor_copy, nc.scalar.copy
+
+        def G(out, in_):
+            nc.gpsimd.tensor_scalar(out=out, in0=in_, scalar1=1.0, scalar2=0.0, op0=ALU.mult, op1=ALU.add)
+
+        for n in range(SWEEP, len(TILES)):
+            for g in range(NG):
+                pass1(n, g)
+            exit1(n)
+        interleave(0, V, 0, B)
+        interleave(1, S, 0, B)
+        add_b4(0, group_tokens(0))
+        quantise_h4(0)
+        add_b4(1, group_tokens(1))
+        turn_tokens(0)
+        b2 = group_tokens(2)
+        quantise_h4(1)
+        add_b4(2, b2)
+        turn_tokens(1)
+        b3 = group_tokens(3)
+        interleave(2, V, 0, 256)
+        interleave(2, S, 256, 512)
+        turn_tokens(2)
+        add_b4(3, b3)
+        for i in range(2):
+            pass2(i, 0)
+            pass2(i, 1)
+        quantise_h4(2, 0, 256)
+        quantise_turned(0)
+        quantise_turned(1)
+        for i in range(2):
+            pass2(i, 2)
+            pass2(i, 3)
+        quantise_h4(2, 256, 512)
+        turn_tokens(3)
+        for i in range(2, 4):
+            pass2(i, 0)
+            pass2(i, 1)
+        finish_add(0)
+        out_pairs(0, G, 0, HALF)
+        quantise_turned(2)
+        finish_add(1)
+        out_pairs(1, S, 0, HALF)
+        quantise_turned(3)
+        for i in range(2, 4):
+            pass2(i, 2)
+            pass2(i, 3)
+        finish_add(2)
+        out_pairs(2, G, 0, HALF)
+        finish_add(3)
+        out_pairs(3, S, 0, 192)
+        out_pairs(3, V, 192, HALF)

@@ -40,12 +40,14 @@ def tile_additivecoupling_pa_w4_kernel(
         make_identity(nc, ident[:])
         w4s = keep.tile([P, NG, MID], U8, name="w4s", align_bytes=64)
         w5s = keep.tile([P, NG, HALF], U8, name="w5s", align_bytes=64)
-        nc.vector.memset(w4s[:].rearrange("p g n -> p (g n)").bitcast(I32), 0)
-        nc.vector.memset(w5s[:].rearrange("p g n -> p (g n)").bitcast(I32), 0)
-        b4rows = keep.tile([P, P], BF16, name="b4rows")
-        nc.gpsimd.memset(b4rows[:], 0.0)
+        srows = keep.tile([P, P], F32, name="srows")
+        nc.vector.memset(srows[:], 0.0)
+        brows = keep.tile([P, P], BF16, name="brows")
+        nc.vector.memset(brows[:], 0.0)
+        nc.gpsimd.memset(w4s[:].rearrange("p g n -> p (g n)").bitcast(I32), 0)
+        nc.gpsimd.memset(w5s[:].rearrange("p g n -> p (g n)").bitcast(I32), 0)
         warm = keep.tile([P, 1], F32, name="warm")
-        nc.gpsimd.memset(warm[:], 0.0)
+        nc.vector.memset(warm[:], 0.0)
         warm2 = keep.tile([P, 1], F32, name="warm2")
         nc.scalar.activation(out=warm2[:], in_=warm[:], func=ACT.Relu)
 
@@ -62,46 +64,41 @@ def tile_additivecoupling_pa_w4_kernel(
             w4a.append(a_g)
         def load_h3(g):
             k_cols = slice(512 * g, 512 * (g + 1))
-            nc.sync.dma_start(out=sc[g][:], in_=h3_scale[:, k_cols].rearrange("o k -> (o k)").partition_broadcast(P))
             nc.sync.dma_start(out=hb[g][:], in_=h3v[:, :, k_cols])
 
         def load_w4(g):
             nc.sync.dma_start(out=w4a[g][:].bitcast(I32), in_=W4_words[g, :, 0 : 1024 * NM].bitcast(I32))
 
+        s0tile = keep.tile([P, 4], F32, name="s0tile")
+        with nc.allow_non_contiguous_dma(reason="512 scales, one to a partition and column"):
+            nc.sync.dma_start(out=s0tile[:], in_=h3_scale[:, 0:512].rearrange("o (m p) -> p (o m)", p=P))
         load_h3(0)
+        nc.sync.dma_start(out=srows[0:16, :], in_=h3_scale.rearrange("o (c p) -> (o c) p", p=P))
         load_h3(1)
+        load_w4(0)
+        nc.sync.dma_start(out=brows[0:16, :], in_=b4.rearrange("(c p) -> c p", p=P))
+        nc.sync.dma_start(out=brows[16:20, :], in_=b5.rearrange("(c p) -> c p", p=P))
+        load_h3(2)
         for q in range(4):
             nc.sync.dma_start(
                 out=w4s[32 * q : 32 * q + 4, :, :].bitcast(I32),
                 in_=W4_scales[:, 4 * q : 4 * q + 4, :].rearrange("g r n -> r g n").bitcast(I32),
             )
-        load_w4(0)
-        load_h3(2)
         load_w4(1)
         load_h3(3)
         load_w4(2)
         load_w4(3)
-        nc.sync.dma_start(out=b4rows[0:16, :], in_=b4.rearrange("(c p) -> c p", p=P))
         nc.sync.dma_start(out=w4b[:].bitcast(I32), in_=W4_words[:, :, 1024 * NM :].rearrange("g p n -> p g n").bitcast(I32))
-        b4bc = keep.tile([P, 512 * (NG - NM)], BF16, name="b4bc")
-        nc.sync.dma_start(out=b4bc[:], in_=b4[512 * NM :].partition_broadcast(P))
+        b4bc = keep.tile([P, 512], F32, name="b4bc")
         for q in range(4):
             nc.sync.dma_start(
                 out=w5s[32 * q : 32 * q + 4, :, :].bitcast(I32),
                 in_=W5_scales[:, 4 * q : 4 * q + 4, :].rearrange("g r n -> r g n").bitcast(I32),
             )
         nc.sync.dma_start(out=w5[:].bitcast(I32), in_=W5_words.rearrange("g p n -> p g n").bitcast(I32))
-        b5bc = keep.tile([P, HALF], BF16, name="b5bc")
-        nc.sync.dma_start(out=b5bc[:], in_=b5.partition_broadcast(P))
+        b5bc = keep.tile([P, HALF], F32, name="b5bc")
         xt = keep.tile([P, TT, 2 * HALF], BF16, name="xt")
         nc.sync.dma_start(out=xt[:], in_=x.rearrange("(p i) c -> p i c", i=TT))
-
-        pair = keep.tile([P, TT, 2, HALF], F32, name="pair")
-        for i in range(TT):
-            nc.gpsimd.tensor_tensor(out=pair[:, i, 0, :], in0=xt[:, i, 0::2], in1=b5bc[:], op=ALU.add)
-            nc.gpsimd.tensor_scalar(
-                out=pair[:, i, 1, :], in0=xt[:, i, 1::2], scalar1=1.0, scalar2=0.0, op0=ALU.mult, op1=ALU.add
-            )
 
         h3g, h3q, h3s, prods = [], [], [], {}
         for g in range(NG):
@@ -154,7 +151,6 @@ def tile_additivecoupling_pa_w4_kernel(
                 stop=(g == NG - 1),
             )
 
-        b4t = keep.tile([P, 16], F32, name="b4t")
         h4n = keep.tile([P, NM, 4, B], BF16, name="h4n", align_bytes=64)
         h4p = []
         for j in range(4):
@@ -166,10 +162,10 @@ def tile_additivecoupling_pa_w4_kernel(
             c = 4 * g + j
             if n in EXIT_V:
                 nc.vector.tensor_scalar(
-                    out=h4p[j][:, g, :], in0=acc[n][:], scalar1=b4t[:, c : c + 1], scalar2=0.0, op0=ALU.add, op1=ALU.max
+                    out=h4p[j][:, g, :], in0=acc[n][:], scalar1=bt[:, c : c + 1], scalar2=0.0, op0=ALU.add, op1=ALU.max
                 )
             else:
-                nc.scalar.activation(out=h4p[j][:, g, :], in_=acc[n][:], func=ACT.Relu, bias=b4t[:, c : c + 1])
+                nc.scalar.activation(out=h4p[j][:, g, :], in_=acc[n][:], func=ACT.Relu, bias=bt[:, c : c + 1])
             moved = {0: None, 1: slice(0, 2), 2: slice(2, 3)}[g]
             if moved is not None:
                 for s in range(4):
@@ -281,12 +277,56 @@ def tile_additivecoupling_pa_w4_kernel(
             if hi == HALF:
                 nc.sync.dma_start(out=outv[:, i, :], in_=outt[i][:].rearrange("p j r -> p (j r)"))
 
-        def turn_b4():
-            b4f = keep.tile([P, P], F32, name="b4f")
-            nc.vector.tensor_copy(out=b4f[:], in_=b4rows[:])
-            b4bank = psum.tile([P, P], F32, name="tr", tag="tr", bufs=2)
-            nc.tensor.transpose(b4bank[:], b4f[:], ident[:])
-            nc.scalar.copy(out=b4t[:], in_=b4bank[:, 0:16])
+        def spread(bank, cols, first):
+            for m in range(4):
+                nc.tensor.transpose(bank[:, m, :], cols[:, first + m : first + m + 1].to_broadcast([P, P]), ident[:])
+
+        def scale_bank(g):
+            bank = psum.tile([P, 4, P], F32, name="acc", tag=f"b{g}", bufs=1)
+            if g == 0:
+                spread(bank, s0tile, 0)
+            else:
+                spread(bank, stile, 4 * g)
+            return bank
+
+        def scale_copy(g, bank, copy):
+            copy(out=sc[g][:], in_=bank[:].rearrange("p m n -> p (m n)"))
+
+        scale_copy(0, scale_bank(0), nc.vector.tensor_copy)
+        stile = keep.tile([P, 16], F32, name="stile")
+        sbank = psum.tile([P, P], F32, name="tr", tag="tr", bufs=2)
+        nc.tensor.transpose(sbank[:], srows[:], ident[:])
+        nc.scalar.copy(out=stile[:], in_=sbank[:, 0:16])
+        scale_copy(1, scale_bank(1), nc.scalar.copy)
+        bt = keep.tile([P, 20], F32, name="bt")
+
+        pair = keep.tile([P, TT, 2, HALF], F32, name="pair")
+
+        def x_pairs():
+            for i in range(TT):
+                nc.gpsimd.tensor_tensor(out=pair[:, i, 0, :], in0=xt[:, i, 0::2], in1=b5bc[:], op=ALU.add)
+                nc.gpsimd.tensor_scalar(
+                    out=pair[:, i, 1, :], in0=xt[:, i, 1::2], scalar1=1.0, scalar2=0.0, op0=ALU.mult, op1=ALU.add
+                )
+
+        def bias_extras(cols, first):
+            bank = psum.tile([P, 4, P], F32, name="tr", tag="tr", bufs=2)
+            spread(bank, bt, first)
+            nc.scalar.copy(out=cols[:], in_=bank[:].rearrange("p m n -> p (m n)"))
+
+        def extras(g):
+            if g == 0:
+                for later in range(2, NG):
+                    scale_copy(later, scale_bank(later), nc.scalar.copy)
+            elif g == 1:
+                browsf = keep.tile([P, P], F32, name="browsf")
+                nc.vector.tensor_copy(out=browsf[:], in_=brows[:])
+                bbank = psum.tile([P, P], F32, name="tr", tag="tr", bufs=2)
+                nc.tensor.transpose(bbank[:], browsf[:], ident[:])
+                nc.scalar.copy(out=bt[:], in_=bbank[:, 0:20])
+            elif g == 2:
+                bias_extras(b5bc, 16)
+                x_pairs()
 
         for g in range(NG):
             product(g, 0)
@@ -297,15 +337,15 @@ def tile_additivecoupling_pa_w4_kernel(
                 quantise_h3(g - 1)
             product(g, 3)
             transpose_pair(g, 1)
+            extras(g)
             if g > 0:
                 for n in range(SWEEP):
                     pass1(n, g - 1)
-            if g == 2:
-                turn_b4()
         quantise_h3(NG - 1)
         for n in range(SWEEP):
             pass1(n, NG - 1)
             exit1(n)
+        bias_extras(b4bc, 12)
         V, S = nc.vector.tensor_copy, nc.scalar.copy
 
         def G(out, in_):

@@ -40,63 +40,59 @@ def tile_additivecoupling_pa_w4_kernel(
         make_identity(nc, ident[:])
         w4s = keep.tile([P, NG, MID], U8, name="w4s", align_bytes=64)
         w5s = keep.tile([P, NG, HALF], U8, name="w5s", align_bytes=64)
+        warm = keep.tile([P, 1], F32, name="warm")
+        nc.vector.memset(warm[:], 0.0)
         srows = keep.tile([P, P], F32, name="srows")
         nc.vector.memset(srows[:], 0.0)
         brows = keep.tile([P, P], BF16, name="brows")
         nc.vector.memset(brows[:], 0.0)
-        nc.gpsimd.memset(w4s[:].rearrange("p g n -> p (g n)").bitcast(I32), 0)
+        nc.vector.memset(w4s[:].rearrange("p g n -> p (g n)").bitcast(I32), 0)
         nc.gpsimd.memset(w5s[:].rearrange("p g n -> p (g n)").bitcast(I32), 0)
-        warm = keep.tile([P, 1], F32, name="warm")
-        nc.vector.memset(warm[:], 0.0)
         warm2 = keep.tile([P, 1], F32, name="warm2")
         nc.scalar.activation(out=warm2[:], in_=warm[:], func=ACT.Relu)
 
         h3v = h3_bytes.rearrange("(p i) k -> p i k", i=TT)
-        sc, hb, w4a = [], [], []
-        w4b = keep.tile([P, NG, 4096 - 1024 * NM], U8, name="w4b", align_bytes=64)
+        hb0 = keep.tile([P, TT, 512], U8, name="hb0", align_bytes=64)
+        hb1 = keep.tile([P, TT, 512], U8, name="hb1", align_bytes=64)
+        hb23 = keep.tile([P, TT, 1024], U8, name="hb23", align_bytes=64)
+        hb = [hb0, hb1, hb23[:, :, 0:512], hb23[:, :, 512:1024]]
+        sc, w4a = [], []
+        w4b = keep.tile([P, NG, 1024], U8, name="w4b", align_bytes=64)
         w5 = keep.tile([P, NG, 1024], U8, name="w5", align_bytes=64)
         for g in range(NG):
             s_g = keep.tile([P, 512], F32, name=f"sc{g}", align_bytes=64)
-            h_g = keep.tile([P, TT, 512], U8, name=f"hb{g}", align_bytes=64)
-            a_g = keep.tile([P, 512 * 2 * NM], U8, name=f"w4a{g}", align_bytes=64)
+            a_g = keep.tile([P, 1024 * NM], U8, name=f"w4a{g}", align_bytes=64)
             sc.append(s_g)
-            hb.append(h_g)
             w4a.append(a_g)
-        def load_h3(g):
-            k_cols = slice(512 * g, 512 * (g + 1))
-            nc.sync.dma_start(out=hb[g][:], in_=h3v[:, :, k_cols])
+        b4bc = keep.tile([P, 512], F32, name="b4bc")
+        b5bc = keep.tile([P, HALF], F32, name="b5bc")
 
         def load_w4(g):
             nc.sync.dma_start(out=w4a[g][:].bitcast(I32), in_=W4_words[g, :, 0 : 1024 * NM].bitcast(I32))
 
+        def load_scales(dst, src):
+            for r in range(4):
+                nc.sync.dma_start(
+                    out=dst[r:P:32, :, :].bitcast(I32), in_=src[:, r:16:4, :].rearrange("g q n -> q g n").bitcast(I32)
+                )
+
         s0tile = keep.tile([P, 4], F32, name="s0tile")
         with nc.allow_non_contiguous_dma(reason="512 scales, one to a partition and column"):
             nc.sync.dma_start(out=s0tile[:], in_=h3_scale[:, 0:512].rearrange("o (m p) -> p (o m)", p=P))
-        load_h3(0)
+        nc.sync.dma_start(out=hb0[:], in_=h3v[:, :, 0:512])
         nc.sync.dma_start(out=srows[0:16, :], in_=h3_scale.rearrange("o (c p) -> (o c) p", p=P))
-        load_h3(1)
-        load_w4(0)
+        nc.sync.dma_start(out=hb1[:], in_=h3v[:, :, 512:1024])
         nc.sync.dma_start(out=brows[0:16, :], in_=b4.rearrange("(c p) -> c p", p=P))
         nc.sync.dma_start(out=brows[16:20, :], in_=b5.rearrange("(c p) -> c p", p=P))
-        load_h3(2)
-        for q in range(4):
-            nc.sync.dma_start(
-                out=w4s[32 * q : 32 * q + 4, :, :].bitcast(I32),
-                in_=W4_scales[:, 4 * q : 4 * q + 4, :].rearrange("g r n -> r g n").bitcast(I32),
-            )
+        load_scales(w4s, W4_scales)
+        load_w4(0)
+        nc.sync.dma_start(out=hb23[:], in_=h3v[:, :, 1024:2048])
         load_w4(1)
-        load_h3(3)
         load_w4(2)
         load_w4(3)
         nc.sync.dma_start(out=w4b[:].bitcast(I32), in_=W4_words[:, :, 1024 * NM :].rearrange("g p n -> p g n").bitcast(I32))
-        b4bc = keep.tile([P, 512], F32, name="b4bc")
-        for q in range(4):
-            nc.sync.dma_start(
-                out=w5s[32 * q : 32 * q + 4, :, :].bitcast(I32),
-                in_=W5_scales[:, 4 * q : 4 * q + 4, :].rearrange("g r n -> r g n").bitcast(I32),
-            )
+        load_scales(w5s, W5_scales)
         nc.sync.dma_start(out=w5[:].bitcast(I32), in_=W5_words.rearrange("g p n -> p g n").bitcast(I32))
-        b5bc = keep.tile([P, HALF], F32, name="b5bc")
         xt = keep.tile([P, TT, 2 * HALF], BF16, name="xt")
         nc.sync.dma_start(out=xt[:], in_=x.rearrange("(p i) c -> p i c", i=TT))
 
@@ -274,8 +270,11 @@ def tile_additivecoupling_pa_w4_kernel(
 
         def out_pairs(i, copy, lo, hi):
             copy(out=outt[i][:, lo:hi, :], in_=pair[:, i, :, lo:hi].rearrange("p r j -> p j r"))
-            if hi == HALF:
-                nc.sync.dma_start(out=outv[:, i, :], in_=outt[i][:].rearrange("p j r -> p (j r)"))
+            start = 0 if i < 3 else lo
+            if hi == HALF or i == 3:
+                nc.sync.dma_start(
+                    out=outv[:, i, 2 * start : 2 * hi], in_=outt[i][:, start:hi, :].rearrange("p j r -> p (j r)")
+                )
 
         def spread(bank, cols, first):
             for m in range(4):
@@ -302,12 +301,9 @@ def tile_additivecoupling_pa_w4_kernel(
 
         pair = keep.tile([P, TT, 2, HALF], F32, name="pair")
 
-        def x_pairs():
-            for i in range(TT):
-                nc.gpsimd.tensor_tensor(out=pair[:, i, 0, :], in0=xt[:, i, 0::2], in1=b5bc[:], op=ALU.add)
-                nc.gpsimd.tensor_scalar(
-                    out=pair[:, i, 1, :], in0=xt[:, i, 1::2], scalar1=1.0, scalar2=0.0, op0=ALU.mult, op1=ALU.add
-                )
+        def x_pairs(i):
+            nc.scalar.activation(out=pair[:, i, 1, :], in_=xt[:, i, 1::2], func=ACT.Copy)
+            nc.vector.tensor_tensor(out=pair[:, i, 0, :], in0=xt[:, i, 0::2], in1=b5bc[:], op=ALU.add)
 
         def bias_extras(cols, first):
             bank = psum.tile([P, 4, P], F32, name="tr", tag="tr", bufs=2)
@@ -326,19 +322,23 @@ def tile_additivecoupling_pa_w4_kernel(
                 nc.scalar.copy(out=bt[:], in_=bbank[:, 0:20])
             elif g == 2:
                 bias_extras(b5bc, 16)
-                x_pairs()
 
         for g in range(NG):
             product(g, 0)
             product(g, 1)
+            if g == 1:
+                quantise_h3(0)
             transpose_pair(g, 0)
+            if g == 1:
+                for n in range(SWEEP):
+                    pass1(n, 0)
             product(g, 2)
-            if g > 0:
+            if g > 1:
                 quantise_h3(g - 1)
             product(g, 3)
             transpose_pair(g, 1)
             extras(g)
-            if g > 0:
+            if g > 1:
                 for n in range(SWEEP):
                     pass1(n, g - 1)
         quantise_h3(NG - 1)
@@ -348,13 +348,12 @@ def tile_additivecoupling_pa_w4_kernel(
         bias_extras(b4bc, 12)
         V, S = nc.vector.tensor_copy, nc.scalar.copy
 
-        def G(out, in_):
-            nc.gpsimd.tensor_scalar(out=out, in0=in_, scalar1=1.0, scalar2=0.0, op0=ALU.mult, op1=ALU.add)
-
         for n in range(SWEEP, len(TILES)):
             for g in range(NG):
                 pass1(n, g)
             exit1(n)
+            if n < SWEEP + TT:
+                x_pairs(n - SWEEP)
         interleave(0, V, 0, B)
         interleave(1, S, 0, B)
         add_b4(0, group_tokens(0))
@@ -385,16 +384,17 @@ def tile_additivecoupling_pa_w4_kernel(
             pass2(i, 0)
             pass2(i, 1)
         finish_add(0)
-        out_pairs(0, G, 0, HALF)
+        out_pairs(0, S, 0, HALF)
         quantise_turned(2)
         finish_add(1)
-        out_pairs(1, S, 0, HALF)
         quantise_turned(3)
+        out_pairs(1, V, 0, HALF)
         for i in range(2, 4):
             pass2(i, 2)
             pass2(i, 3)
         finish_add(2)
-        out_pairs(2, G, 0, HALF)
+        out_pairs(2, S, 0, 256)
+        out_pairs(2, V, 256, HALF)
         finish_add(3)
-        out_pairs(3, S, 0, 192)
-        out_pairs(3, V, 192, HALF)
+        out_pairs(3, S, 0, 256)
+        out_pairs(3, V, 256, HALF)

@@ -21,7 +21,7 @@ ALU = mybir.AluOpType
 ACT = mybir.ActivationFunctionType
 
 NM = 3
-TILES = [(g, j) for j in range(4) for g in range(2)] + [(2, j) for j in range(4)]
+TILES = [(g, j) for g in range(NM) for j in range(4)]
 SWEEP = 6
 EXIT_V = (1, 3, 5, 7, 9)
 
@@ -61,9 +61,11 @@ def tile_additivecoupling_pa_w4_kernel(
         w5 = keep.tile([P, NG, 1024], U8, name="w5", align_bytes=64)
         for g in range(NG):
             s_g = keep.tile([P, 512], F32, name=f"sc{g}", align_bytes=64)
-            a_g = keep.tile([P, 1024 * NM], U8, name=f"w4a{g}", align_bytes=64)
             sc.append(s_g)
-            w4a.append(a_g)
+        w4a0 = keep.tile([P, 1024 * NM], U8, name="w4a0", align_bytes=64)
+        w4a1 = keep.tile([P, 1024 * NM], U8, name="w4a1", align_bytes=64)
+        w4a23 = keep.tile([P, 2, 1024 * NM], U8, name="w4a23", align_bytes=64)
+        w4a = [w4a0, w4a1, w4a23[:, 0, :], w4a23[:, 1, :]]
         b4bc = keep.tile([P, 512], F32, name="b4bc")
         b5bc = keep.tile([P, HALF], F32, name="b5bc")
 
@@ -82,14 +84,15 @@ def tile_additivecoupling_pa_w4_kernel(
         nc.sync.dma_start(out=hb0[:], in_=h3v[:, :, 0:512])
         nc.sync.dma_start(out=srows[0:16, :], in_=h3_scale.rearrange("o (c p) -> (o c) p", p=P))
         nc.sync.dma_start(out=hb1[:], in_=h3v[:, :, 512:1024])
-        nc.sync.dma_start(out=brows[0:16, :], in_=b4.rearrange("(c p) -> c p", p=P))
-        nc.sync.dma_start(out=brows[16:20, :], in_=b5.rearrange("(c p) -> c p", p=P))
+        nc.gpsimd.dma_start(out=brows[0:16, :], in_=b4.rearrange("(c p) -> c p", p=P))
+        nc.gpsimd.dma_start(out=brows[16:20, :], in_=b5.rearrange("(c p) -> c p", p=P))
         load_scales(w4s, W4_scales)
-        load_w4(0)
         nc.sync.dma_start(out=hb23[:], in_=h3v[:, :, 1024:2048])
+        load_w4(0)
         load_w4(1)
-        load_w4(2)
-        load_w4(3)
+        nc.sync.dma_start(
+            out=w4a23[:].bitcast(I32), in_=W4_words[2:4, :, 0 : 1024 * NM].rearrange("g p n -> p g n").bitcast(I32)
+        )
         nc.sync.dma_start(out=w4b[:].bitcast(I32), in_=W4_words[:, :, 1024 * NM :].rearrange("g p n -> p g n").bitcast(I32))
         load_scales(w5s, W5_scales)
         nc.sync.dma_start(out=w5[:].bitcast(I32), in_=W5_words.rearrange("g p n -> p g n").bitcast(I32))
@@ -147,25 +150,22 @@ def tile_additivecoupling_pa_w4_kernel(
                 stop=(g == NG - 1),
             )
 
-        h4n = keep.tile([P, NM, 4, B], BF16, name="h4n", align_bytes=64)
-        h4p = []
-        for j in range(4):
-            t_j = keep.tile([P, NM, B], BF16, name=f"h4p{j}", align_bytes=64)
-            h4p.append(t_j)
+        h4n = []
+        for g in range(NM):
+            t_g = keep.tile([P, 4, B], BF16, name=f"h4n{g}", align_bytes=64)
+            h4n.append(t_g)
 
         def exit1(n):
             g, j = TILES[n]
             c = 4 * g + j
+            h4 = work.tile([P, B], BF16, name="h4", tag="h4", bufs=12, align_bytes=64)
             if n in EXIT_V:
                 nc.vector.tensor_scalar(
-                    out=h4p[j][:, g, :], in0=acc[n][:], scalar1=bt[:, c : c + 1], scalar2=0.0, op0=ALU.add, op1=ALU.max
+                    out=h4[:], in0=acc[n][:], scalar1=bt[:, c : c + 1], scalar2=0.0, op0=ALU.add, op1=ALU.max
                 )
             else:
-                nc.scalar.activation(out=h4p[j][:, g, :], in_=acc[n][:], func=ACT.Relu, bias=bt[:, c : c + 1])
-            moved = {0: None, 1: slice(0, 2), 2: slice(2, 3)}[g]
-            if moved is not None:
-                for s in range(4):
-                    nc.sync.dma_start(out=h4n[32 * j : 32 * (j + 1), moved, s, :], in_=h4p[j][s:P:4, moved, :])
+                nc.scalar.activation(out=h4[:], in_=acc[n][:], func=ACT.Relu, bias=bt[:, c : c + 1])
+            nc.sync.dma_start(out=h4n[g][32 * j : 32 * (j + 1), :, :].rearrange("a s c -> a (s c)"), in_=h4[:])
 
         h4q, h4s = [], []
         for g in range(NG):
@@ -180,7 +180,7 @@ def tile_additivecoupling_pa_w4_kernel(
             if g not in inter:
                 t = work.tile([P, B, 4], BF16, name="h4i", tag="h4i", bufs=3, align_bytes=64)
                 inter[g] = t
-            copy(out=inter[g][:, lo:hi, :], in_=h4n[:, g, :, lo:hi].rearrange("p t c -> p c t"))
+            copy(out=inter[g][:, lo:hi, :], in_=h4n[g][:, :, lo:hi].rearrange("p t c -> p c t"))
 
         def quantise_h4(g, lo=0, hi=B):
             nc.vector.quantize_mx(
@@ -326,26 +326,21 @@ def tile_additivecoupling_pa_w4_kernel(
         for g in range(NG):
             product(g, 0)
             product(g, 1)
-            if g == 1:
-                quantise_h3(0)
             transpose_pair(g, 0)
-            if g == 1:
-                for n in range(SWEEP):
-                    pass1(n, 0)
             product(g, 2)
-            if g > 1:
+            if g > 0:
                 quantise_h3(g - 1)
             product(g, 3)
             transpose_pair(g, 1)
             extras(g)
-            if g > 1:
+            if g > 0:
                 for n in range(SWEEP):
                     pass1(n, g - 1)
+        bias_extras(b4bc, 12)
         quantise_h3(NG - 1)
         for n in range(SWEEP):
             pass1(n, NG - 1)
             exit1(n)
-        bias_extras(b4bc, 12)
         V, S = nc.vector.tensor_copy, nc.scalar.copy
 
         for n in range(SWEEP, len(TILES)):
@@ -354,41 +349,46 @@ def tile_additivecoupling_pa_w4_kernel(
             exit1(n)
             if n < SWEEP + TT:
                 x_pairs(n - SWEEP)
-        interleave(0, V, 0, B)
-        interleave(1, S, 0, B)
-        add_b4(0, group_tokens(0))
+            if n == 9:
+                interleave(0, V, 0, 256)
+                interleave(0, S, 256, B)
         quantise_h4(0)
+        add_b4(0, group_tokens(0))
+        interleave(1, V, 0, 256)
+        interleave(1, S, 256, B)
         add_b4(1, group_tokens(1))
-        turn_tokens(0)
-        b2 = group_tokens(2)
         quantise_h4(1)
-        add_b4(2, b2)
+        add_b4(2, group_tokens(2))
+        turn_tokens(0)
         turn_tokens(1)
         b3 = group_tokens(3)
+        add_b4(3, b3)
         interleave(2, V, 0, 256)
         interleave(2, S, 256, 512)
-        turn_tokens(2)
-        add_b4(3, b3)
         for i in range(2):
             pass2(i, 0)
             pass2(i, 1)
+        turn_tokens(2)
+        turn_tokens(3)
         quantise_h4(2, 0, 256)
         quantise_turned(0)
         quantise_turned(1)
+        quantise_h4(2, 256, 512)
+        pass2(2, 0)
+        pass2(2, 1)
         for i in range(2):
             pass2(i, 2)
             pass2(i, 3)
-        quantise_h4(2, 256, 512)
-        turn_tokens(3)
-        for i in range(2, 4):
-            pass2(i, 0)
-            pass2(i, 1)
-        finish_add(0)
-        out_pairs(0, S, 0, HALF)
+        pass2(3, 0)
+        pass2(3, 1)
         quantise_turned(2)
-        finish_add(1)
         quantise_turned(3)
-        out_pairs(1, V, 0, HALF)
+        finish_add(0)
+        out_pairs(0, S, 0, 256)
+        out_pairs(0, V, 256, HALF)
+        finish_add(1)
+        out_pairs(1, S, 0, 256)
+        out_pairs(1, V, 256, HALF)
         for i in range(2, 4):
             pass2(i, 2)
             pass2(i, 3)

@@ -66,8 +66,8 @@ def tile_additivecoupling_pa_w4_kernel(
         w4a1 = keep.tile([P, 1024 * NM], U8, name="w4a1", align_bytes=64)
         w4a23 = keep.tile([P, 2, 1024 * NM], U8, name="w4a23", align_bytes=64)
         w4a = [w4a0, w4a1, w4a23[:, 0, :], w4a23[:, 1, :]]
-        b4bc = keep.tile([P, 512], F32, name="b4bc")
-        b5bc = keep.tile([P, HALF], F32, name="b5bc")
+        b4bc = keep.tile([P, 512], BF16, name="b4bc")
+        b5bc = keep.tile([P, HALF], BF16, name="b5bc")
 
         def load_w4(g):
             nc.sync.dma_start(out=w4a[g][:].bitcast(I32), in_=W4_words[g, :, 0 : 1024 * NM].bitcast(I32))
@@ -84,11 +84,10 @@ def tile_additivecoupling_pa_w4_kernel(
         nc.sync.dma_start(out=hb0[:], in_=h3v[:, :, 0:512])
         nc.sync.dma_start(out=srows[0:16, :], in_=h3_scale.rearrange("o (c p) -> (o c) p", p=P))
         nc.sync.dma_start(out=hb1[:], in_=h3v[:, :, 512:1024])
-        nc.gpsimd.dma_start(out=brows[0:16, :], in_=b4.rearrange("(c p) -> c p", p=P))
-        nc.gpsimd.dma_start(out=brows[16:20, :], in_=b5.rearrange("(c p) -> c p", p=P))
         load_scales(w4s, W4_scales)
         nc.sync.dma_start(out=hb23[:], in_=h3v[:, :, 1024:2048])
         load_w4(0)
+        nc.sync.dma_start(out=brows[0:12, :], in_=b4[0 : 512 * NM].rearrange("(c p) -> c p", p=P))
         load_w4(1)
         nc.sync.dma_start(
             out=w4a23[:].bitcast(I32), in_=W4_words[2:4, :, 0 : 1024 * NM].rearrange("g p n -> p g n").bitcast(I32)
@@ -97,7 +96,9 @@ def tile_additivecoupling_pa_w4_kernel(
         load_scales(w5s, W5_scales)
         nc.sync.dma_start(out=w5[:].bitcast(I32), in_=W5_words.rearrange("g p n -> p g n").bitcast(I32))
         xt = keep.tile([P, TT, 2 * HALF], BF16, name="xt")
+        nc.sync.dma_start(out=b5bc[:], in_=b5.partition_broadcast(P))
         nc.sync.dma_start(out=xt[:], in_=x.rearrange("(p i) c -> p i c", i=TT))
+        nc.sync.dma_start(out=b4bc[:], in_=b4[512 * NM :].partition_broadcast(P))
 
         h3g, h3q, h3s, prods = [], [], [], {}
         for g in range(NG):
@@ -297,7 +298,7 @@ def tile_additivecoupling_pa_w4_kernel(
         nc.tensor.transpose(sbank[:], srows[:], ident[:])
         nc.scalar.copy(out=stile[:], in_=sbank[:, 0:16])
         scale_copy(1, scale_bank(1), nc.scalar.copy)
-        bt = keep.tile([P, 20], F32, name="bt")
+        bt = keep.tile([P, 12], F32, name="bt")
 
         pair = keep.tile([P, TT, 2, HALF], F32, name="pair")
 
@@ -305,38 +306,30 @@ def tile_additivecoupling_pa_w4_kernel(
             nc.scalar.activation(out=pair[:, i, 1, :], in_=xt[:, i, 1::2], func=ACT.Copy)
             nc.vector.tensor_tensor(out=pair[:, i, 0, :], in0=xt[:, i, 0::2], in1=b5bc[:], op=ALU.add)
 
-        def bias_extras(cols, first):
-            bank = psum.tile([P, 4, P], F32, name="tr", tag="tr", bufs=2)
-            spread(bank, bt, first)
-            nc.scalar.copy(out=cols[:], in_=bank[:].rearrange("p m n -> p (m n)"))
-
-        def extras(g):
-            if g == 0:
-                for later in range(2, NG):
-                    scale_copy(later, scale_bank(later), nc.scalar.copy)
-            elif g == 1:
-                browsf = keep.tile([P, P], F32, name="browsf")
-                nc.vector.tensor_copy(out=browsf[:], in_=brows[:])
-                bbank = psum.tile([P, P], F32, name="tr", tag="tr", bufs=2)
-                nc.tensor.transpose(bbank[:], browsf[:], ident[:])
-                nc.scalar.copy(out=bt[:], in_=bbank[:, 0:20])
-            elif g == 2:
-                bias_extras(b5bc, 16)
+        def turn_b4():
+            browsf = keep.tile([P, P], F32, name="browsf")
+            nc.gpsimd.tensor_copy(out=browsf[:], in_=brows[:])
+            bbank = psum.tile([P, P], F32, name="tr", tag="tr", bufs=2)
+            nc.tensor.transpose(bbank[:], browsf[:], ident[:])
+            nc.scalar.copy(out=bt[:], in_=bbank[:, 0:12])
 
         for g in range(NG):
+            if g == 2:
+                turn_b4()
             product(g, 0)
             product(g, 1)
             transpose_pair(g, 0)
             product(g, 2)
+            product(g, 3)
             if g > 0:
                 quantise_h3(g - 1)
-            product(g, 3)
             transpose_pair(g, 1)
-            extras(g)
+            if g == 0:
+                for later in range(2, NG):
+                    scale_copy(later, scale_bank(later), nc.scalar.copy)
             if g > 0:
                 for n in range(SWEEP):
                     pass1(n, g - 1)
-        bias_extras(b4bc, 12)
         quantise_h3(NG - 1)
         for n in range(SWEEP):
             pass1(n, NG - 1)
@@ -374,16 +367,15 @@ def tile_additivecoupling_pa_w4_kernel(
         quantise_turned(0)
         quantise_turned(1)
         quantise_h4(2, 256, 512)
-        pass2(2, 0)
-        pass2(2, 1)
         for i in range(2):
             pass2(i, 2)
             pass2(i, 3)
-        pass2(3, 0)
-        pass2(3, 1)
+        for i in range(2, 4):
+            pass2(i, 0)
+            pass2(i, 1)
         quantise_turned(2)
-        quantise_turned(3)
         finish_add(0)
+        quantise_turned(3)
         out_pairs(0, S, 0, 256)
         out_pairs(0, V, 256, HALF)
         finish_add(1)

from contextlib import ExitStack

import concourse.mybir as mybir
from concourse.masks import make_identity

B, HALF, MID = 512, 512, 2048
FLOPS = 2 * B * MID * MID + 2 * B * MID * HALF

P = 128
TT = B // P
NG = MID // 512
F32 = mybir.dt.float32
BF16 = mybir.dt.bfloat16
U8 = mybir.dt.uint8
U32 = mybir.dt.uint32
I32 = mybir.dt.int32
FP8 = mybir.dt.float8_e4m3fn
FP8X4 = mybir.dt.float8_e4m3fn_x4
FP4X4 = mybir.dt.float4_e2m1fn_x4
ALU = mybir.AluOpType
ACT = mybir.ActivationFunctionType

NM = 3
TILES = [(g, j) for g in range(NM) for j in range(4)]
SWEEP = 6
EXIT_V = (1, 3, 5, 7, 9)


def tile_additivecoupling_pa_w4_kernel(
    tc, x, h3_bytes, h3_scale, W4_words, W4_scales, b4, W5_words, W5_scales, b5, out
):
    nc = tc.nc
    with ExitStack() as ctx:
        keep = ctx.enter_context(tc.tile_pool(name="keep", bufs=1))
        work = ctx.enter_context(tc.tile_pool(name="work", bufs=2))
        psum = ctx.enter_context(tc.psum_pool(name="psum", bufs=1))
        ctx.enter_context(tc.manual_schedule())

        ident = keep.tile([P, P], F32, name="ident")
        make_identity(nc, ident[:])
        w4s = keep.tile([P, NG, MID], U8, name="w4s", align_bytes=64)
        w5s = keep.tile([P, NG, HALF], U8, name="w5s", align_bytes=64)
        warm = keep.tile([P, 1], F32, name="warm")
        nc.vector.memset(warm[:], 0.0)
        srows = keep.tile([P, P], F32, name="srows")
        nc.vector.memset(srows[:], 0.0)
        brows = keep.tile([P, P], BF16, name="brows")
        nc.vector.memset(brows[:], 0.0)
        nc.vector.memset(w4s[:].rearrange("p g n -> p (g n)").bitcast(I32), 0)
        nc.gpsimd.memset(w5s[:].rearrange("p g n -> p (g n)").bitcast(I32), 0)
        warm2 = keep.tile([P, 1], F32, name="warm2")
        nc.scalar.activation(out=warm2[:], in_=warm[:], func=ACT.Relu)

        h3v = h3_bytes.rearrange("(p i) k -> p i k", i=TT)
        hb0 = keep.tile([P, TT, 512], U8, name="hb0", align_bytes=64)
        hb1 = keep.tile([P, TT, 512], U8, name="hb1", align_bytes=64)
        hb23 = keep.tile([P, TT, 1024], U8, name="hb23", align_bytes=64)
        hb = [hb0, hb1, hb23[:, :, 0:512], hb23[:, :, 512:1024]]
        sc, w4a = [], []
        w4b = keep.tile([P, NG, 1024], U8, name="w4b", align_bytes=64)
        w5 = keep.tile([P, NG, 1024], U8, name="w5", align_bytes=64)
        for g in range(NG):
            s_g = keep.tile([P, 512], F32, name=f"sc{g}", align_bytes=64)
            sc.append(s_g)
        w4a0 = keep.tile([P, 1024 * NM], U8, name="w4a0", align_bytes=64)
        w4a1 = keep.tile([P, 1024 * NM], U8, name="w4a1", align_bytes=64)
        w4a23 = keep.tile([P, 2, 1024 * NM], U8, name="w4a23", align_bytes=64)
        w4a = [w4a0, w4a1, w4a23[:, 0, :], w4a23[:, 1, :]]
        b4bc = keep.tile([P, 512], BF16, name="b4bc")
        b5bc = keep.tile([P, HALF], BF16, name="b5bc")

        def load_w4(g):
            nc.sync.dma_start(out=w4a[g][:].bitcast(I32), in_=W4_words[g, :, 0 : 1024 * NM].bitcast(I32))

        def load_scales(dst, src):
            for r in range(4):
                nc.sync.dma_start(
                    out=dst[r:P:32, :, :].bitcast(I32), in_=src[:, r:16:4, :].rearrange("g q n -> q g n").bitcast(I32)
                )

        s0tile = keep.tile([P, 4], F32, name="s0tile")
        with nc.allow_non_contiguous_dma(reason="512 scales, one to a partition and column"):
            nc.sync.dma_start(out=s0tile[:], in_=h3_scale[:, 0:512].rearrange("o (m p) -> p (o m)", p=P))
        nc.sync.dma_start(out=hb0[:], in_=h3v[:, :, 0:512])
        nc.sync.dma_start(out=srows[0:16, :], in_=h3_scale.rearrange("o (c p) -> (o c) p", p=P))
        nc.sync.dma_start(out=hb1[:], in_=h3v[:, :, 512:1024])
        load_scales(w4s, W4_scales)
        nc.sync.dma_start(out=hb23[:], in_=h3v[:, :, 1024:2048])
        load_w4(0)
        nc.sync.dma_start(out=brows[0:12, :], in_=b4[0 : 512 * NM].rearrange("(c p) -> c p", p=P))
        load_w4(1)
        nc.sync.dma_start(
            out=w4a23[:].bitcast(I32), in_=W4_words[2:4, :, 0 : 1024 * NM].rearrange("g p n -> p g n").bitcast(I32)
        )
        nc.sync.dma_start(out=w4b[:].bitcast(I32), in_=W4_words[:, :, 1024 * NM :].rearrange("g p n -> p g n").bitcast(I32))
        load_scales(w5s, W5_scales)
        nc.sync.dma_start(out=w5[:].bitcast(I32), in_=W5_words.rearrange("g p n -> p g n").bitcast(I32))
        xt = keep.tile([P, TT, 2 * HALF], BF16, name="xt")
        nc.sync.dma_start(out=b5bc[:], in_=b5.partition_broadcast(P))
        nc.sync.dma_start(out=xt[:], in_=x.rearrange("(p i) c -> p i c", i=TT))
        nc.sync.dma_start(out=b4bc[:], in_=b4[512 * NM :].partition_broadcast(P))

        h3g, h3q, h3s, prods = [], [], [], {}
        for g in range(NG):
            t_g = work.tile([P, B, 4], BF16, name="h3g", tag="h3g", bufs=2, align_bytes=64)
            q_g = keep.tile([P, B], U32, name=f"h3q{g}", align_bytes=64)
            s_g = keep.tile([P, B], U8, name=f"h3s{g}", align_bytes=64)
            h3g.append(t_g)
            h3q.append(q_g)
            h3s.append(s_g)

        def product(g, i):
            t = work.tile([P, 512], BF16, name="prod", tag="prod", bufs=6, align_bytes=64)
            nc.vector.tensor_tensor(out=t[:], in0=hb[g][:, i, :].bitcast(FP8), in1=sc[g][:], op=ALU.mult)
            prods[g, i] = t

        def transpose_pair(g, half):
            bank = psum.tile([P, 2, 2, P], F32, name="tr", tag="tr", bufs=2)
            for ii in range(2):
                words = prods[g, 2 * half + ii][:].bitcast(F32)
                for u in range(2):
                    nc.tensor.transpose(bank[:, ii, u, :], words[:, u::2], ident[:])
            dst = h3g[g][:, 256 * half : 256 * (half + 1), :].rearrange("p c t -> p (c t)").bitcast(F32)
            nc.scalar.copy(
                out=dst.rearrange("p (i m u) -> p i m u", i=2, u=2), in_=bank[:].rearrange("p i u m -> p i m u")
            )

        def quantise_h3(g):
            cols = slice(0, B)
            nc.vector.quantize_mx(
                out=h3q[g][:, cols].bitcast(FP8X4),
                scales=h3s[g][:, cols],
                in_=h3g[g][:, cols, :].rearrange("p c t -> p (c t)"),
            )

        acc = {}

        def pass1(n, g):
            if g == 0:
                bank = psum.tile([P, B], F32, name="acc", tag=f"b{n % 6}", bufs=1)
                acc[n] = bank
            c = 4 * TILES[n][0] + TILES[n][1]
            w = w4a[g][:, 256 * c : 256 * (c + 1)]
            nc.tensor.matmul_mx(
                out=acc[n][:],
                lhsT=w.bitcast(FP4X4),
                lhsT_scale=w4s[:, g, P * c : P * (c + 1)],
                rhs=h3q[g][:].bitcast(FP8X4),
                rhs_scale=h3s[g][:],
                start=(g == 0),
                stop=(g == NG - 1),
            )

        h4n = []
        for g in range(NM):
            t_g = keep.tile([P, 4, B], BF16, name=f"h4n{g}", align_bytes=64)
            h4n.append(t_g)

        def exit1(n):
            g, j = TILES[n]
            c = 4 * g + j
            h4 = work.tile([P, B], BF16, name="h4", tag="h4", bufs=12, align_bytes=64)
            if n in EXIT_V:
                nc.vector.tensor_scalar(
                    out=h4[:], in0=acc[n][:], scalar1=bt[:, c : c + 1], scalar2=0.0, op0=ALU.add, op1=ALU.max
                )
            else:
                nc.scalar.activation(out=h4[:], in_=acc[n][:], func=ACT.Relu, bias=bt[:, c : c + 1])
            nc.sync.dma_start(out=h4n[g][32 * j : 32 * (j + 1), :, :].rearrange("a s c -> a (s c)"), in_=h4[:])

        h4q, h4s = [], []
        for g in range(NG):
            q_g = keep.tile([P, B], U32, name=f"h4q{g}", align_bytes=64)
            s_g = keep.tile([P, B], U8, name=f"h4s{g}", align_bytes=64)
            h4q.append(q_g)
            h4s.append(s_g)

        inter = {}

        def interleave(g, copy, lo, hi):
            if g not in inter:
                t = work.tile([P, B, 4], BF16, name="h4i", tag="h4i", bufs=3, align_bytes=64)
                inter[g] = t
            copy(out=inter[g][:, lo:hi, :], in_=h4n[g][:, :, lo:hi].rearrange("p t c -> p c t"))

        def quantise_h4(g, lo=0, hi=B):
            nc.vector.quantize_mx(
                out=h4q[g][:, lo:hi].bitcast(FP8X4),
                scales=h4s[g][:, lo:hi],
                in_=inter[g][:, lo:hi, :].rearrange("p c t -> p (c t)"),
            )

        h4t = {}

        def group_tokens(i):
            o = 3
            bank = psum.tile([P, 512], F32, name="acc", tag=f"b{i % 2}", bufs=1)
            cols = slice(P * i, P * (i + 1))
            for g in range(NG):
                nc.tensor.matmul_mx(
                    out=bank[:],
                    lhsT=h3q[g][:, cols].bitcast(FP8X4),
                    lhsT_scale=h3s[g][:, cols],
                    rhs=w4b[:, g, 1024 * (o - NM) : 1024 * (o - NM + 1)].bitcast(FP4X4),
                    rhs_scale=w4s[:, g, 512 * o : 512 * (o + 1)],
                    start=(g == 0),
                    stop=(g == NG - 1),
                )
            return bank

        def add_b4(i, bank):
            t = work.tile([P, 512], BF16, name="h4t", tag="h4t", bufs=4, align_bytes=64)
            order = "q (p u e) -> q u p e"
            nc.vector.tensor_tensor(
                out=t[:].rearrange("q (u p e) -> q u p e", u=2, e=2),
                in0=bank[:].rearrange(order, u=2, e=2),
                in1=b4bc[:].rearrange(order, u=2, e=2),
                op=ALU.add,
            )
            h4t[i] = t

        turned = {}

        def turn_tokens(i):
            bank = psum.tile([P, 2, P], F32, name="tr", tag="tr", bufs=2)
            words = h4t[i][:].bitcast(F32)
            for u in range(2):
                nc.tensor.transpose(bank[:, u, :], words[:, P * u : P * (u + 1)], ident[:])
            r = work.tile([P, P, 4], BF16, name="h4r", tag="h4r", bufs=4, align_bytes=64)
            nc.scalar.activation(
                out=r[:].rearrange("p m (u e) -> p m u e", u=2),
                in_=bank[:].rearrange("p u m -> p (u m)").bitcast(BF16).rearrange("p (u m e) -> p m u e", u=2, e=2),
                func=ACT.Relu,
            )
            turned[i] = r

        def quantise_turned(i):
            cols = slice(P * i, P * (i + 1))
            nc.vector.quantize_mx(
                out=h4q[3][:, cols].bitcast(FP8X4),
                scales=h4s[3][:, cols],
                in_=turned[i][:].rearrange("p m t -> p (m t)"),
            )

        acc2 = {}

        def pass2(i, g):
            if g == 0:
                bank = psum.tile([P, HALF], F32, name="acc", tag=f"b{2 + i}", bufs=1)
                acc2[i] = bank
            cols = slice(P * i, P * (i + 1))
            nc.tensor.matmul_mx(
                out=acc2[i][:],
                lhsT=h4q[g][:, cols].bitcast(FP8X4),
                lhsT_scale=h4s[g][:, cols],
                rhs=w5[:, g, :].bitcast(FP4X4),
                rhs_scale=w5s[:, g, :],
                start=(g == 0),
                stop=(g == NG - 1),
            )

        outv = out.rearrange("(p i) c -> p i c", i=TT)

        outt = []
        for i in range(TT):
            o_i = keep.tile([P, HALF, 2], F32, name=f"o{i}")
            outt.append(o_i)

        def finish_add(i):
            nc.vector.tensor_tensor(out=pair[:, i, 0, :], in0=acc2[i][:], in1=pair[:, i, 0, :], op=ALU.add)

        def out_pairs(i, copy, lo, hi):
            copy(out=outt[i][:, lo:hi, :], in_=pair[:, i, :, lo:hi].rearrange("p r j -> p j r"))
            start = 0 if i < 3 else lo
            if hi == HALF or i == 3:
                nc.sync.dma_start(
                    out=outv[:, i, 2 * start : 2 * hi], in_=outt[i][:, start:hi, :].rearrange("p j r -> p (j r)")
                )

        def spread(bank, cols, first):
            for m in range(4):
                nc.tensor.transpose(bank[:, m, :], cols[:, first + m : first + m + 1].to_broadcast([P, P]), ident[:])

        def scale_bank(g):
            bank = psum.tile([P, 4, P], F32, name="acc", tag=f"b{g}", bufs=1)
            if g == 0:
                spread(bank, s0tile, 0)
            else:
                spread(bank, stile, 4 * g)
            return bank

        def scale_copy(g, bank, copy):
            copy(out=sc[g][:], in_=bank[:].rearrange("p m n -> p (m n)"))

        scale_copy(0, scale_bank(0), nc.vector.tensor_copy)
        stile = keep.tile([P, 16], F32, name="stile")
        sbank = psum.tile([P, P], F32, name="tr", tag="tr", bufs=2)
        nc.tensor.transpose(sbank[:], srows[:], ident[:])
        nc.scalar.copy(out=stile[:], in_=sbank[:, 0:16])
        scale_copy(1, scale_bank(1), nc.scalar.copy)
        bt = keep.tile([P, 12], F32, name="bt")

        pair = keep.tile([P, TT, 2, HALF], F32, name="pair")

        def x_pairs(i):
            nc.scalar.activation(out=pair[:, i, 1, :], in_=xt[:, i, 1::2], func=ACT.Copy)
            nc.vector.tensor_tensor(out=pair[:, i, 0, :], in0=xt[:, i, 0::2], in1=b5bc[:], op=ALU.add)

        def turn_b4():
            browsf = keep.tile([P, P], F32, name="browsf")
            nc.gpsimd.tensor_copy(out=browsf[:], in_=brows[:])
            bbank = psum.tile([P, P], F32, name="tr", tag="tr", bufs=2)
            nc.tensor.transpose(bbank[:], browsf[:], ident[:])
            nc.scalar.copy(out=bt[:], in_=bbank[:, 0:12])

        for g in range(NG):
            if g == 2:
                turn_b4()
            product(g, 0)
            product(g, 1)
            transpose_pair(g, 0)
            product(g, 2)
            product(g, 3)
            if g > 0:
                quantise_h3(g - 1)
            transpose_pair(g, 1)
            if g == 0:
                for later in range(2, NG):
                    scale_copy(later, scale_bank(later), nc.scalar.copy)
            if g > 0:
                for n in range(SWEEP):
                    pass1(n, g - 1)
        quantise_h3(NG - 1)
        for n in range(SWEEP):
            pass1(n, NG - 1)
            exit1(n)
        V, S = nc.vector.tensor_copy, nc.scalar.copy

        for n in range(SWEEP, len(TILES)):
            for g in range(NG):
                pass1(n, g)
            exit1(n)
            if n < SWEEP + TT:
                x_pairs(n - SWEEP)
            if n == 9:
                interleave(0, V, 0, 256)
                interleave(0, S, 256, B)
        quantise_h4(0)
        add_b4(0, group_tokens(0))
        interleave(1, V, 0, 256)
        interleave(1, S, 256, B)
        add_b4(1, group_tokens(1))
        quantise_h4(1)
        add_b4(2, group_tokens(2))
        turn_tokens(0)
        turn_tokens(1)
        b3 = group_tokens(3)
        add_b4(3, b3)
        interleave(2, V, 0, 256)
        interleave(2, S, 256, 512)
        for i in range(2):
            pass2(i, 0)
            pass2(i, 1)
        turn_tokens(2)
        turn_tokens(3)
        quantise_h4(2, 0, 256)
        quantise_turned(0)
        quantise_turned(1)
        quantise_h4(2, 256, 512)
        for i in range(2):
            pass2(i, 2)
            pass2(i, 3)
        for i in range(2, 4):
            pass2(i, 0)
            pass2(i, 1)
        quantise_turned(2)
        finish_add(0)
        quantise_turned(3)
        out_pairs(0, S, 0, 256)
        out_pairs(0, V, 256, HALF)
        finish_add(1)
        out_pairs(1, S, 0, 256)
        out_pairs(1, V, 256, HALF)
        for i in range(2, 4):
            pass2(i, 2)
            pass2(i, 3)
        finish_add(2)
        out_pairs(2, S, 0, 256)
        out_pairs(2, V, 256, HALF)
        finish_add(3)
        out_pairs(3, S, 0, 256)
        out_pairs(3, V, 256, HALF)
